import numpy as np
import ml_dtypes


def mxq(x, axis, fmt="e4m3"):
    dtype, down = {"e4m3": (ml_dtypes.float8_e4m3fn, 7), "e5m2": (ml_dtypes.float8_e5m2, 14)}[fmt]
    v = np.moveaxis(np.asarray(x, np.float32).astype(ml_dtypes.bfloat16).astype(np.float64), axis, -1)
    blocks = v.reshape(v.shape[:-1] + (-1, 32))
    amax = np.abs(blocks).max(-1, keepdims=True)
    byte = np.maximum(np.where(amax > 0, np.frexp(amax)[1] - 1 + 127, 0) - down, 1)
    scale = np.exp2(byte - 127.0)
    codes = (blocks / scale).astype(np.float32).astype(dtype).astype(np.float64)
    return np.moveaxis((codes * scale).reshape(v.shape), -1, axis)


WIDE = False


def mx_kscale(k):
    if not WIDE:
        return np.ones(k)
    levels = np.array([10, -10, 5, -5, 0])
    if k % 512:
        return np.exp2(np.random.permutation(np.resize(levels, k // 32))).repeat(32)
    a = np.empty((k // 512, 16))
    for p in range(k // 512):
        a[p, :8] = np.random.permutation(np.resize(levels, 8))
        for g in range(8):
            far = levels[np.abs(levels - a[p, g]) >= 10]
            a[p, g + 8] = far[np.random.randint(len(far))]
    return np.exp2(a.ravel()).repeat(32)


BF16 = ml_dtypes.bfloat16


def bf(x):
    return np.asarray(x, np.float32).astype(BF16)


def f64(x):
    return np.asarray(x).astype(np.float64)


E2M1 = np.array([0.0, 0.5, 1.0, 1.5, 2.0, 3.0, 4.0, 6.0, -0.0, -0.5, -1.0, -1.5, -2.0, -3.0, -4.0, -6.0])


def pack_weight(w, fmt):
    k, n = w.shape
    w = f64(bf(w)).reshape(k // 32, 32, n)
    amax = np.abs(w).max(1)
    if fmt == "e4m3":
        byte = np.frexp(amax)[1] - 1 + 127 - 7
    else:
        mant, ex = np.frexp(amax / 6.0)
        byte = np.where(mant > 0.5, ex, ex - 1) + 127
    byte = np.clip(np.where(amax > 0, byte, 1), 1, 254)
    scaled = (w * np.exp2(127.0 - byte)[:, None, :]).reshape(k, n).astype(np.float32)
    by_word = np.ascontiguousarray(scaled.reshape(k // 512, 128, 4, n).transpose(0, 1, 3, 2))
    if fmt == "e4m3":
        words = by_word.astype(ml_dtypes.float8_e4m3fn).view(np.uint8)
    else:
        c = by_word.astype(ml_dtypes.float4_e2m1fn).view(np.uint8) & 0xF
        words = c[..., 0::2] | (c[..., 1::2] << 4)
    return np.ascontiguousarray(words), np.ascontiguousarray(byte.astype(np.uint8).reshape(k // 512, 16, n))


def unpack_weight(words, scales, fmt):
    g, p, n, _ = words.shape
    if fmt == "e4m3":
        vals = np.ascontiguousarray(words).view(ml_dtypes.float8_e4m3fn).astype(np.float64)
    else:
        nib = np.empty((g, p, n, 4), np.uint8)
        nib[..., 0::2] = words & 0xF
        nib[..., 1::2] = words >> 4
        vals = E2M1[nib]
    vals = vals * np.repeat(np.exp2(scales.astype(np.float64) - 127.0), 8, axis=1)[..., None]
    return vals.transpose(0, 1, 3, 2).reshape(g * 512, n)
def pack4(w):
    words, scales = pack_weight(w, "e2m1")
    return words.reshape(words.shape[0], 128, -1), scales


def unpack4(words, scales):
    return unpack_weight(words.reshape(words.shape[0], 128, -1, 2), scales, "e2m1")


B, S, DIM, N_HEADS, Q_LORA, KV_LORA, NOPE, ROPE, V_HEAD = 1, 512, 2048, 16, 1536, 512, 128, 64, 128
HV = N_HEADS * V_HEAD


def draw0():
    s, t = mx_kscale(KV_LORA), mx_kscale(HV)
    o_lat = bf(np.random.standard_normal((B, S, N_HEADS, KV_LORA)) * 0.35 * s)
    w_uv = bf(np.random.standard_normal((N_HEADS, V_HEAD, KV_LORA)) * 2.0 / np.sqrt(KV_LORA) / s * t.reshape(N_HEADS, V_HEAD, 1))
    wo_words, wo_scales = pack4((np.random.standard_normal((DIM, HV)) / np.sqrt(HV) / t).T)
    return {"o_lat": o_lat,
            "w_uv": w_uv,
            "wo_words": wo_words,
            "wo_scales": wo_scales}


def core(o_lat, w_uv, wo_words, wo_scales):
    ol = mxq(f64(o_lat), 3, "e4m3").transpose(0, 2, 1, 3)
    wv = mxq(f64(w_uv), 2, "e4m3").transpose(0, 2, 1)
    o = ol @ wv[None]
    o = o.transpose(0, 2, 1, 3).reshape(B, S, HV)
    return mxq(o, 2, "e4m3") @ unpack4(wo_words, wo_scales)


def e4m3fn_bytes(y):
    return np.clip(np.asarray(y, np.float64), -448.0, 448.0).astype(np.float32).astype(ml_dtypes.float8_e4m3fn).view(np.uint8)


def e4m3fn_values(b):
    return np.asarray(b, np.uint8).view(ml_dtypes.float8_e4m3fn).astype(np.float64)


def setup_inputs():
    d = draw0()
    x0 = np.asarray(d['o_lat']).astype(np.float64)
    s = (np.max(np.abs(x0), axis=(0, 1, 2), keepdims=True) / 448.0).astype(np.float32)
    out = {}
    for k, v in d.items():
        if k == 'o_lat':
            out['o_lat_bytes'] = e4m3fn_bytes(x0 / s.astype(np.float64))
            out['o_lat_scale'] = s
        else:
            out[k] = v
    return out


def reference(o_lat_bytes, o_lat_scale, w_uv, wo_words, wo_scales):
    return core(e4m3fn_values(o_lat_bytes) * o_lat_scale.astype(np.float64), w_uv, wo_words, wo_scales)

from contextlib import ExitStack

import concourse.mybir as mybir
from concourse.masks import make_identity

FLOPS = 2 * 512 * 16 * 512 * 128 + 2 * 512 * 2048 * 2048

F32 = mybir.dt.float32
BF16 = mybir.dt.bfloat16
U32 = mybir.dt.uint32
I32 = mybir.dt.int32
U8 = mybir.dt.uint8
FP8 = mybir.dt.float8_e4m3fn
E4 = mybir.dt.float8_e4m3fn_x4
E2 = mybir.dt.float4_e2m1fn_x4
MULT = mybir.AluOpType.mult

P = 128
PERM = False


def tile_mla_pc_w4_kernel(tc, o_lat_bytes, o_lat_scale, w_uv, wo_words, wo_scales, out):
    nc = tc.nc
    xin = o_lat_bytes.rearrange("o (m s) h c -> m s (o h c)", s=P)
    wuv_in = w_uv.rearrange("(g h) d c -> g d h c", h=4)
    out_v = out.rearrange("o (m s) n -> m s (o n)", s=P)

    with ExitStack() as ctx:
        keep = ctx.enter_context(tc.tile_pool(name="keep", bufs=1))
        work = ctx.enter_context(tc.tile_pool(name="work", bufs=3))
        ps_t = ctx.enter_context(tc.psum_pool(name="ps_t", bufs=2))
        ps_a = ctx.enter_context(tc.psum_pool(name="ps_a", bufs=1))
        ps_acc = ctx.enter_context(tc.psum_pool(name="ps_acc", bufs=1))

        ident = keep.tile([P, P], F32, name="ident", align_bytes=64)
        make_identity(nc, ident[:])
        scale = keep.tile([P, 2048], F32, name="scale", align_bytes=64)
        wos = keep.tile([P, 4, 2048], U8, name="wos", align_bytes=64)
        wow = keep.tile([P, 4, 4096], U8, name="wow", align_bytes=64)
        xraw = [[keep.tile([P, 2048], U8, name="xraw%d_%d" % (m, g), align_bytes=64) for g in range(4)] for m in range(4)]
        wraw = [keep.tile([P, 4, 512], BF16, name="wraw%d" % g, align_bytes=64) for g in range(4)]
        wcodes = [keep.tile([P, 512], U32, name="wcodes%d" % g, align_bytes=64) for g in range(4)]
        wscales = [keep.tile([P, 512], U8, name="wscales%d" % g, align_bytes=64) for g in range(4)]

        nc.vector.memset(wos[:].rearrange("p g n -> p (g n)").bitcast(I32), 0)

        def load_x(m, g):
            nc.sync.dma_start(out=xraw[m][g][:], in_=xin[m][:, g * 2048:(g + 1) * 2048])

        def load_w(g):
            nc.sync.dma_start(out=wraw[g][:], in_=wuv_in[g])

        nc.sync.dma_start(out=scale[:, 0:512], in_=o_lat_scale.rearrange("a b c k -> (a b c k)").partition_broadcast(P))
        load_x(0, 0)
        load_w(0)
        for g in range(1, 4):
            load_x(0, g)
            load_w(g)
        for g in range(4):
            load_x(1, g)
        for g in range(4):
            nc.sync.dma_start(out=wow[:, g, :].bitcast(I32), in_=wo_words[g].bitcast(I32))
        wos_i = wos[:].rearrange("p g n -> p (g n)").bitcast(I32).rearrange("p (g n) -> p g n", g=4)
        for q in range(4):
            nc.sync.dma_start(
                out=wos_i[32 * q:32 * q + 4],
                in_=wo_scales[:, 4 * q:4 * q + 4, :].rearrange("g q n -> q g n").bitcast(I32),
            )
        for m in (2, 3):
            for g in range(4):
                load_x(m, g)

        for r in range(1, 4):
            nc.vector.tensor_copy(out=scale[:, 512 * r:512 * (r + 1)], in_=scale[:, 0:512])

        xb = {}
        tp = {}
        tt = {}
        codes = {}
        accs = {}

        def W(i):
            m, g = divmod(i, 4)
            t = work.tile([P, 2048], BF16, name="xb", align_bytes=64)
            src = xraw[m][g][:].bitcast(FP8)
            if PERM:
                for h in range(4):
                    cols = slice(512 * h, 512 * (h + 1))
                    nc.vector.tensor_tensor(
                        out=t[:, cols].rearrange("p (u b i) -> p b u i", u=2, b=16),
                        in0=src[:, cols].rearrange("p (b u i) -> p b u i", u=2, b=16),
                        in1=scale[:, 0:512].rearrange("p (b u i) -> p b u i", u=2, b=16),
                        op=MULT)
            else:
                nc.vector.tensor_tensor(out=t[:], in0=src, in1=scale[:], op=MULT)
            xb[i] = t[:]

        def WP(g):
            if PERM:
                t = work.tile([P, 2048], BF16, name="wb", align_bytes=64)
                for h in range(4):
                    nc.vector.tensor_copy(
                        out=t[:, 512 * h:512 * (h + 1)].rearrange("p (u b i) -> p u b i", u=2, b=16),
                        in_=wraw[g][:, h, :].rearrange("p (b u i) -> p u b i", u=2, b=16))
                xb["w%d" % g] = t[:]
            else:
                xb["w%d" % g] = wraw[g][:].rearrange("p h c -> p (h c)")

        def T(key):
            words = xb[key].bitcast(F32)
            banks = []
            for half in range(2):
                ps = ps_t.tile([P, 2, 2, P], F32, name="psT")
                for hh in range(2):
                    h = 2 * half + hh
                    for u in range(2):
                        if PERM:
                            w = words[:, 256 * h + 128 * u:256 * h + 128 * (u + 1)]
                        else:
                            w = words[:, 256 * h + u:256 * (h + 1):2]
                        nc.tensor.transpose(ps[:, hh, u, :], w, ident[:])
                banks.append(ps)
            tp[key] = banks

        def X(key):
            t = work.tile([P, 4, P, 4], BF16, name="xt", align_bytes=64)
            tw = t[:].rearrange("p h r t -> p (h r t)").bitcast(F32)
            for half in range(2):
                nc.scalar.copy(
                    out=tw[:, 512 * half:512 * (half + 1)].rearrange("p (h r u) -> p h r u", h=2, u=2),
                    in_=tp[key][half][:].rearrange("p h u r -> p h r u"))
            tt[key] = t

        def Q(key):
            if isinstance(key, str):
                g = int(key[1:])
                c, s = wcodes[g], wscales[g]
            else:
                c = work.tile([P, 512], U32, name="xcodes", align_bytes=64)
                s = work.tile([P, 512], U8, name="xscales", align_bytes=64)
            nc.vector.quantize_mx(out=c[:].bitcast(E4), scales=s[:], in_=tt[key][:].rearrange("p h r t -> p (h r t)"))
            codes[key] = (c, s)

        pa = {}
        ob = {}
        po = {}
        oi = {}
        oc = {}

        def A(i):
            g = i % 4
            ps = ps_a.tile([P, 512], F32, name="psA")
            c, s = codes[i]
            for h in range(4):
                cols = slice(128 * h, 128 * (h + 1))
                nc.tensor.matmul_mx(out=ps[:, cols], lhsT=c[:, cols].bitcast(E4), lhsT_scale=s[:, cols],
                                    rhs=wcodes[g][:, cols].bitcast(E4), rhs_scale=wscales[g][:, cols], start=True, stop=True)
            pa[i] = ps

        def B(i):
            t = work.tile([P, 512], BF16, name="ob", align_bytes=64)
            nc.scalar.copy(out=t[:].rearrange("p (u w e) -> p u w e", u=2, e=2),
                           in_=pa[i][:].rearrange("p (w u e) -> p u w e", u=2, e=2))
            ob[i] = t

        def O(i):
            ps = ps_a.tile([P, 2, P], F32, name="psO")
            words = ob[i][:].bitcast(F32)
            for u in range(2):
                nc.tensor.transpose(ps[:, u, :], words[:, 128 * u:128 * (u + 1)], ident[:])
            po[i] = ps

        def Cc(i):
            t = work.tile([P, 512], BF16, name="oi", align_bytes=64)
            nc.scalar.copy(out=t[:].bitcast(F32).rearrange("p (r u) -> p r u", u=2), in_=po[i][:].rearrange("p u r -> p r u"))
            oi[i] = t

        def R(i):
            c = work.tile([P, 128], U32, name="ocodes", align_bytes=64)
            s = work.tile([P, 128], U8, name="oscales", align_bytes=64)
            nc.vector.quantize_mx(out=c[:].bitcast(E4), scales=s[:], in_=oi[i][:])
            oc[i] = (c, s)

        def M(i):
            m, g = divmod(i, 4)
            c, s = oc[i]
            for n in range(4):
                if g == 0:
                    accs[n] = ps_acc.tile([P, 512], F32, name="acc%d" % n)
                nc.tensor.matmul_mx(out=accs[n][:], lhsT=c[:].bitcast(E4), lhsT_scale=s[:],
                                    rhs=wow[:, g, 1024 * n:1024 * (n + 1)].bitcast(E2), rhs_scale=wos[:, g, 512 * n:512 * (n + 1)],
                                    start=(g == 0), stop=(g == 3))

        def E(m):
            for n in range(4):
                t = work.tile([P, 512], F32, name="res%d" % n)
                if m == 3 and n % 2:
                    nc.vector.tensor_copy(out=t[:], in_=accs[n][:])
                else:
                    nc.scalar.copy(out=t[:], in_=accs[n][:])
                nc.sync.dma_start(out=out_v[m][:, 512 * n:512 * (n + 1)], in_=t[:])

        with tc.manual_schedule():
            WP(0)
            T("w0")
            X("w0")
            W(0)
            Q("w0")
            for i in range(16 + 4):
                if i < 16:
                    T(i)
                    X(i)
                if 0 <= i - 2 < 16:
                    O(i - 2)
                if 1 <= i + 1 < 4:
                    WP(i + 1)
                if 0 <= i - 3 < 16:
                    R(i - 3)
                if i + 1 < 16:
                    W(i + 1)
                if 0 <= i - 1 < 16:
                    A(i - 1)
                    B(i - 1)
                if 0 <= i - 2 < 16:
                    Cc(i - 2)
                if 1 <= i + 1 < 4:
                    T("w%d" % (i + 1))
                    X("w%d" % (i + 1))
                if i < 16:
                    Q(i)
                if 1 <= i + 1 < 4:
                    Q("w%d" % (i + 1))
                if 0 <= i - 3 < 16:
                    M(i - 3)
                    if (i - 3) % 4 == 3:
                        E((i - 3) // 4)
